import numpy as np
import ml_dtypes


def mxq(x, axis, fmt="e4m3"):
    dtype, down = {"e4m3": (ml_dtypes.float8_e4m3fn, 7), "e5m2": (ml_dtypes.float8_e5m2, 14)}[fmt]
    v = np.moveaxis(np.asarray(x, np.float32).astype(ml_dtypes.bfloat16).astype(np.float64), axis, -1)
    blocks = v.reshape(v.shape[:-1] + (-1, 32))
    amax = np.abs(blocks).max(-1, keepdims=True)
    byte = np.maximum(np.where(amax > 0, np.frexp(amax)[1] - 1 + 127, 0) - down, 1)
    scale = np.exp2(byte - 127.0)
    codes = (blocks / scale).astype(np.float32).astype(dtype).astype(np.float64)
    return np.moveaxis((codes * scale).reshape(v.shape), -1, axis)


WIDE = False


def mx_kscale(k):
    if not WIDE:
        return np.ones(k)
    levels = np.array([10, -10, 5, -5, 0])
    a = np.random.permutation(np.resize(levels, k // 512 * 4)).reshape(k // 512, 4)
    idx = np.arange(k)
    return np.exp2(a[idx // 512, idx % 128 // 32])


BF16 = ml_dtypes.bfloat16


def bf(x):
    return np.asarray(x, np.float32).astype(BF16)


def f64(x):
    return np.asarray(x).astype(np.float64)


N, NFEAT, NHEADS, NHID, NCLASS = 4096, 512, 4, 32, 128
P = 0.08


def elu(v):
    return np.where(v > 0, v, np.exp(np.minimum(v, 0.0)) - 1.0)


def setup_inputs():
    s, t = mx_kscale(NFEAT), mx_kscale(N)
    edges = np.random.random((N, N)) < P
    return {"x": bf(np.random.standard_normal((N, NFEAT)) * s / t[:, None]),
            "adj": bf(edges * (0.5 + np.random.random((N, N))) * t),
            "W0": bf(np.random.standard_normal((NHEADS, NFEAT, NHID)) * 1.5 / np.sqrt(NFEAT * P * N) / s[:, None])}


def reference(x, adj, W0):
    h = mxq(f64(x), 1, "e4m3") @ mxq(f64(W0), 1, "e4m3")
    hp = mxq(f64(adj), 1, "e4m3") @ mxq(h, 1, "e4m3")
    return elu(hp).transpose(1, 0, 2).reshape(N, NHEADS * NHID)

@@ -1,0 +1,209 @@
+from contextlib import ExitStack
+
+import concourse.mybir as mybir
+from concourse.masks import make_identity
+
+BF16 = mybir.dt.bfloat16
+F32 = mybir.dt.float32
+U32 = mybir.dt.uint32
+U8 = mybir.dt.uint8
+FP8X4 = mybir.dt.float8_e4m3fn_x4
+ACT = mybir.ActivationFunctionType
+ALU = mybir.AluOpType
+
+P = 128
+PACK = 4
+K_PASS = P * PACK
+
+NODES = 4096
+FEATURES = 512
+OUT_COLS = 128
+
+SLAB_COLS = 4096
+CHUNKS = SLAB_COLS // K_PASS
+BANK_WORDS = 512
+SLAB_BANKS = SLAB_COLS // 2 // BANK_WORDS
+BANK_CHUNKS = CHUNKS // SLAB_BANKS
+
+X_SLABS = NODES * FEATURES // (P * SLAB_COLS)
+ADJ_SLABS = NODES // P
+SLABS = X_SLABS + ADJ_SLABS
+BLOCK_SLABS = 4
+
+RUN = 1
+ROWS_BUFS = 10
+
+FLOPS = 2 * NODES * FEATURES * OUT_COLS + 2 * NODES * NODES * OUT_COLS
+
+
+def tile_gat_pa_t_kernel(tc, x, adj, W0, out):
+    nc = tc.nc
+
+    x_view = x.rearrange("(j p e) f -> p j (e f)", p=P, e=2)
+    x_runs = SLAB_COLS // (2 * FEATURES)
+    w_view = W0.flatten_outer_dims().rearrange("(c q e) f -> q c (e f)", q=P, e=2)
+
+    with ExitStack() as stack:
+        const = stack.enter_context(tc.tile_pool(name="const", bufs=1))
+        rows_pool = stack.enter_context(tc.tile_pool(name="rows", bufs=ROWS_BUFS))
+        grouped_pool = stack.enter_context(tc.tile_pool(name="grouped", bufs=2 * RUN + 1))
+        codes_pool = stack.enter_context(tc.tile_pool(name="codes", bufs=2 * RUN + 1))
+        elu_pool = stack.enter_context(tc.tile_pool(name="elu", bufs=2))
+        turned_psum = stack.enter_context(tc.psum_pool(name="turned", bufs=6))
+        sums_psum = stack.enter_context(tc.psum_pool(name="sums", bufs=2))
+        stack.enter_context(tc.manual_schedule())
+
+        rows_of = {}
+        grouped_of = {}
+        codes_of = {}
+        scales_of = {}
+        sums_of = {}
+        exp_of = {}
+
+        def load(s):
+            rows = rows_pool.tile([P, SLAB_COLS], BF16)
+            if s < X_SLABS:
+                nc.sync.dma_start(
+                    out=rows[:].rearrange("p (j c) -> p j c", j=x_runs),
+                    in_=x_view[:, s * x_runs : (s + 1) * x_runs, :],
+                )
+            else:
+                block, i = divmod(s - X_SLABS, BLOCK_SLABS)
+                block_rows = adj[block * BLOCK_SLABS * P : (block + 1) * BLOCK_SLABS * P, :]
+                nc.sync.dma_start(
+                    out=rows[:],
+                    in_=block_rows.rearrange("(p i) k -> p i k", i=BLOCK_SLABS)[:, i, :],
+                )
+            rows_of[s] = rows
+
+        def turn(s):
+            words = rows_of[s][:].bitcast(F32)
+            grouped = grouped_pool.tile([P, SLAB_COLS], BF16, align_bytes=64)
+            grouped_words = grouped[:].bitcast(F32)
+            for b in range(SLAB_BANKS):
+                turned = turned_psum.tile([P, 2 * BANK_CHUNKS, P], F32)
+                for j in range(2 * BANK_CHUNKS):
+                    first = (b * 2 * BANK_CHUNKS + j) * P
+                    nc.tensor.transpose(turned[:, j, :], words[:, first : first + P], ident[:])
+                copy = nc.vector.tensor_copy if b == 0 else nc.scalar.copy
+                copy(
+                    out=grouped_words[:, b * BANK_WORDS : (b + 1) * BANK_WORDS].rearrange(
+                        "p (c r u) -> p c r u", c=BANK_CHUNKS, u=2
+                    ),
+                    in_=turned[:].rearrange("p (c u) r -> p c r u", u=2),
+                )
+            grouped_of[s] = grouped
+
+        def quantise(s):
+            codes = codes_pool.tile([P, CHUNKS * P], U32, align_bytes=64)
+            scales = codes_pool.tile([P, CHUNKS * P], U8, align_bytes=64)
+            nc.vector.quantize_mx(
+                out=codes[:].bitcast(FP8X4), scales=scales[:], in_=grouped_of[s][:]
+            )
+            codes_of[s] = codes
+            scales_of[s] = scales
+
+        def mx_pass(s, c, acc, rhs_codes, rhs_scales, start, stop):
+            cols = slice(c * P, (c + 1) * P)
+            nc.tensor.matmul_mx(
+                out=acc,
+                lhsT=codes_of[s][:, cols].bitcast(FP8X4),
+                lhsT_scale=scales_of[s][:, cols],
+                rhs=rhs_codes.bitcast(FP8X4),
+                rhs_scale=rhs_scales,
+                start=start,
+                stop=stop,
+            )
+
+        def project(s):
+            for half in range(2):
+                g_pass = 2 * s + half
+                g_sums = sums_psum.tile([P, PACK, OUT_COLS], F32, tag="sums")
+                for t in range(PACK):
+                    mx_pass(s, PACK * half + t, g_sums[:, t, :], w_codes[:], w_scales[:], True, True)
+                copy = nc.vector.tensor_copy if half == 0 else nc.scalar.copy
+                copy(out=g_grouped[:, g_pass, :, :], in_=g_sums[:].rearrange("p t c -> p c t"))
+
+        def quantise_g(s):
+            cols = slice(2 * s * OUT_COLS, (2 * s + 2) * OUT_COLS)
+            nc.vector.quantize_mx(
+                out=g_codes[:, cols].bitcast(FP8X4),
+                scales=g_scales[:, cols],
+                in_=g_grouped[:, 2 * s : 2 * s + 2, :, :].rearrange("p g c t -> p (g c t)"),
+            )
+
+        def aggregate(s):
+            block, i = divmod(s - X_SLABS, BLOCK_SLABS)
+            if i == 0:
+                sums = sums_psum.tile([P, BLOCK_SLABS, OUT_COLS], F32, tag="sums")
+                sums_of[block] = sums
+            sums = sums_of[block]
+            for c in range(CHUNKS):
+                cols = slice(c * OUT_COLS, (c + 1) * OUT_COLS)
+                mx_pass(s, c, sums[:, i, :], g_codes[:, cols], g_scales[:, cols], c == 0, c == CHUNKS - 1)
+            if i == BLOCK_SLABS - 1:
+                v = sums[:].rearrange("p i c -> p (i c)")
+                minus_min = elu_pool.tile([P, BLOCK_SLABS * OUT_COLS], F32)
+                nc.scalar.activation(out=minus_min[:], in_=v, func=ACT.Relu, scale=-1.0)
+                exp_min = elu_pool.tile([P, BLOCK_SLABS * OUT_COLS], F32)
+                nc.scalar.activation(out=exp_min[:], in_=minus_min[:], func=ACT.Exp, scale=-1.0)
+                exp_of[block] = exp_min
+
+        def finish(s):
+            block, i = divmod(s - X_SLABS, BLOCK_SLABS)
+            if i == BLOCK_SLABS - 1:
+                result = elu_pool.tile([P, BLOCK_SLABS * OUT_COLS], F32)
+                nc.vector.scalar_tensor_tensor(
+                    out=result[:],
+                    in0=exp_of[block][:],
+                    scalar=-1.0,
+                    in1=sums_of[block][:].rearrange("p i c -> p (i c)"),
+                    op0=ALU.add,
+                    op1=ALU.max,
+                )
+                block_out = out[block * BLOCK_SLABS * P : (block + 1) * BLOCK_SLABS * P, :]
+                nc.sync.dma_start(
+                    out=block_out.rearrange("(p i) c -> p (i c)", i=BLOCK_SLABS), in_=result[:]
+                )
+
+        w_raw = const.tile([P, 2 * 4, 2 * 32], BF16)
+        nc.scalar.dma_start(out=w_raw[:], in_=w_view)
+        for s in range(ROWS_BUFS):
+            load(s)
+        ident = const.tile([P, P], F32)
+        make_identity(nc, ident[:])
+        w_grouped = const.tile([P, OUT_COLS, PACK], BF16, align_bytes=64)
+        for h in range(4):
+            nc.vector.tensor_copy(
+                out=w_grouped[:, 32 * h : 32 * (h + 1), :].rearrange("q f (v e) -> q f v e", v=2),
+                in_=w_raw[:, 2 * h : 2 * (h + 1), :].rearrange("q v (e f) -> q f v e", e=2),
+            )
+        w_codes = const.tile([P, OUT_COLS], U32, align_bytes=64)
+        w_scales = const.tile([P, OUT_COLS], U8, align_bytes=64)
+        nc.vector.quantize_mx(
+            out=w_codes[:].bitcast(FP8X4),
+            scales=w_scales[:],
+            in_=w_grouped[:].rearrange("q c t -> q (c t)"),
+        )
+        g_grouped = const.tile([P, CHUNKS, OUT_COLS, PACK], BF16, align_bytes=64)
+        g_codes = const.tile([P, CHUNKS * OUT_COLS], U32, align_bytes=64)
+        g_scales = const.tile([P, CHUNKS * OUT_COLS], U8, align_bytes=64)
+
+        for first in range(0, SLABS + 3 * RUN, RUN):
+            for s in range(first, first + RUN):
+                if s < SLABS:
+                    turn(s)
+                    if s + ROWS_BUFS < SLABS:
+                        load(s + ROWS_BUFS)
+                if 0 <= s - RUN < SLABS:
+                    quantise(s - RUN)
+            for s in range(first - 3 * RUN, first - 2 * RUN):
+                if 0 <= s < X_SLABS:
+                    quantise_g(s)
+                elif X_SLABS <= s < SLABS:
+                    finish(s)
+            for s in range(first - 2 * RUN, first - RUN):
+                if 0 <= s < X_SLABS:
+                    project(s)
+                elif X_SLABS <= s < SLABS:
+                    aggregate(s)

@@ -29,6 +29,7 @@ X_SLABS = NODES * FEATURES // (P * SLAB_COLS)
 ADJ_SLABS = NODES // P
 SLABS = X_SLABS + ADJ_SLABS
 BLOCK_SLABS = 4
+BLOCKS = ADJ_SLABS // BLOCK_SLABS
 
 RUN = 1
 ROWS_BUFS = 10
@@ -152,19 +153,21 @@ def tile_gat_pa_t_kernel(tc, x, adj, W0, out):
         def finish(s):
             block, i = divmod(s - X_SLABS, BLOCK_SLABS)
             if i == BLOCK_SLABS - 1:
-                result = elu_pool.tile([P, BLOCK_SLABS * OUT_COLS], F32)
                 nc.vector.scalar_tensor_tensor(
-                    out=result[:],
+                    out=results[:, block, :],
                     in0=exp_of[block][:],
                     scalar=-1.0,
                     in1=sums_of[block][:].rearrange("p i c -> p (i c)"),
                     op0=ALU.add,
                     op1=ALU.max,
                 )
-                block_out = out[block * BLOCK_SLABS * P : (block + 1) * BLOCK_SLABS * P, :]
-                nc.sync.dma_start(
-                    out=block_out.rearrange("(p i) c -> p (i c)", i=BLOCK_SLABS), in_=result[:]
-                )
+
+        def store(block):
+            block_out = out[block * BLOCK_SLABS * P : (block + 1) * BLOCK_SLABS * P, :]
+            nc.sync.dma_start(
+                out=block_out.rearrange("(p i) c -> p (i c)", i=BLOCK_SLABS),
+                in_=results[:, block, :],
+            )
 
         w_raw = const.tile([P, 2 * 4, 2 * 32], BF16)
         nc.scalar.dma_start(out=w_raw[:], in_=w_view)
@@ -188,6 +191,7 @@ def tile_gat_pa_t_kernel(tc, x, adj, W0, out):
         g_grouped = const.tile([P, CHUNKS, OUT_COLS, PACK], BF16, align_bytes=64)
         g_codes = const.tile([P, CHUNKS * OUT_COLS], U32, align_bytes=64)
         g_scales = const.tile([P, CHUNKS * OUT_COLS], U8, align_bytes=64)
+        results = const.tile([P, BLOCKS, BLOCK_SLABS * OUT_COLS], F32)
 
         for first in range(0, SLABS + 3 * RUN, RUN):
             for s in range(first, first + RUN):
@@ -207,3 +211,6 @@ def tile_gat_pa_t_kernel(tc, x, adj, W0, out):
                     project(s)
                 elif X_SLABS <= s < SLABS:
                     aggregate(s)
+
+        for block in range(BLOCKS):
+            store(block)

@@ -17,12 +17,15 @@ K_PASS = P * PACK
 
 NODES = 4096
 FEATURES = 512
-OUT_COLS = 128
+HEADS = 4
+HIDDEN = 32
+OUT_COLS = HEADS * HIDDEN
 
 SLAB_COLS = 4096
 CHUNKS = SLAB_COLS // K_PASS
 BANK_WORDS = 512
 SLAB_BANKS = SLAB_COLS // 2 // BANK_WORDS
+BANK_COLS = SLAB_COLS // SLAB_BANKS
 BANK_CHUNKS = CHUNKS // SLAB_BANKS
 
 X_SLABS = NODES * FEATURES // (P * SLAB_COLS)
@@ -31,10 +34,21 @@ SLABS = X_SLABS + ADJ_SLABS
 BLOCK_SLABS = 4
 BLOCKS = ADJ_SLABS // BLOCK_SLABS
 
-RUN = 1
+RUN = 2
 ROWS_BUFS = 10
 
 FLOPS = 2 * NODES * FEATURES * OUT_COLS + 2 * NODES * NODES * OUT_COLS
+
+
+def group_of(a):
+    first = a - a % BLOCK_SLABS
+    last = first + BLOCK_SLABS - 1
+    if last == ADJ_SLABS - 1:
+        if a == last:
+            first = last
+        else:
+            last = last - 1
+    return first, last
 
 
 def tile_gat_pa_t_kernel(tc, x, adj, W0, out):
@@ -47,15 +61,14 @@ def tile_gat_pa_t_kernel(tc, x, adj, W0, out):
     with ExitStack() as stack:
         const = stack.enter_context(tc.tile_pool(name="const", bufs=1))
         rows_pool = stack.enter_context(tc.tile_pool(name="rows", bufs=ROWS_BUFS))
-        grouped_pool = stack.enter_context(tc.tile_pool(name="grouped", bufs=2 * RUN + 1))
-        codes_pool = stack.enter_context(tc.tile_pool(name="codes", bufs=2 * RUN + 1))
+        grouped_pool = stack.enter_context(tc.tile_pool(name="grouped", bufs=3))
+        codes_pool = stack.enter_context(tc.tile_pool(name="codes", bufs=RUN + 2))
         elu_pool = stack.enter_context(tc.tile_pool(name="elu", bufs=2))
         turned_psum = stack.enter_context(tc.psum_pool(name="turned", bufs=6))
         sums_psum = stack.enter_context(tc.psum_pool(name="sums", bufs=2))
         stack.enter_context(tc.manual_schedule())
 
         rows_of = {}
-        grouped_of = {}
         codes_of = {}
         scales_of = {}
         sums_of = {}
@@ -63,24 +76,30 @@ def tile_gat_pa_t_kernel(tc, x, adj, W0, out):
 
         def load(s):
             rows = rows_pool.tile([P, SLAB_COLS], BF16)
+            rows_of[s] = rows
             if s < X_SLABS:
                 nc.sync.dma_start(
                     out=rows[:].rearrange("p (j c) -> p j c", j=x_runs),
                     in_=x_view[:, s * x_runs : (s + 1) * x_runs, :],
                 )
-            else:
-                block, i = divmod(s - X_SLABS, BLOCK_SLABS)
-                block_rows = adj[block * BLOCK_SLABS * P : (block + 1) * BLOCK_SLABS * P, :]
-                nc.sync.dma_start(
-                    out=rows[:],
-                    in_=block_rows.rearrange("(p i) k -> p i k", i=BLOCK_SLABS)[:, i, :],
-                )
-            rows_of[s] = rows
+                return
+            block, i = divmod(s - X_SLABS, BLOCK_SLABS)
+            block_rows = adj[block * BLOCK_SLABS * P : (block + 1) * BLOCK_SLABS * P, :]
+            slab_rows = block_rows.rearrange("(p i) k -> p i k", i=BLOCK_SLABS)[:, i, :]
+            pieces = SLAB_BANKS if s == SLABS - 1 else 1
+            width = SLAB_COLS // pieces
+            for piece in range(pieces):
+                cols = slice(piece * width, (piece + 1) * width)
+                nc.sync.dma_start(out=rows[:, cols], in_=slab_rows[:, cols])
 
         def turn(s):
             words = rows_of[s][:].bitcast(F32)
             grouped = grouped_pool.tile([P, SLAB_COLS], BF16, align_bytes=64)
             grouped_words = grouped[:].bitcast(F32)
+            codes = codes_pool.tile([P, CHUNKS * P], U32, align_bytes=64)
+            scales = codes_pool.tile([P, CHUNKS * P], U8, align_bytes=64)
+            codes_of[s] = codes
+            scales_of[s] = scales
             for b in range(SLAB_BANKS):
                 turned = turned_psum.tile([P, 2 * BANK_CHUNKS, P], F32)
                 for j in range(2 * BANK_CHUNKS):
@@ -93,16 +112,13 @@ def tile_gat_pa_t_kernel(tc, x, adj, W0, out):
                     ),
                     in_=turned[:].rearrange("p (c u) r -> p c r u", u=2),
                 )
-            grouped_of[s] = grouped
-
-        def quantise(s):
-            codes = codes_pool.tile([P, CHUNKS * P], U32, align_bytes=64)
-            scales = codes_pool.tile([P, CHUNKS * P], U8, align_bytes=64)
-            nc.vector.quantize_mx(
-                out=codes[:].bitcast(FP8X4), scales=scales[:], in_=grouped_of[s][:]
-            )
-            codes_of[s] = codes
-            scales_of[s] = scales
+            for b in range(SLAB_BANKS):
+                cols = slice(b * BANK_CHUNKS * P, (b + 1) * BANK_CHUNKS * P)
+                nc.vector.quantize_mx(
+                    out=codes[:, cols].bitcast(FP8X4),
+                    scales=scales[:, cols],
+                    in_=grouped[:, b * BANK_COLS : (b + 1) * BANK_COLS],
+                )
 
         def mx_pass(s, c, acc, rhs_codes, rhs_scales, start, stop):
             cols = slice(c * P, (c + 1) * P)
@@ -118,14 +134,11 @@ def tile_gat_pa_t_kernel(tc, x, adj, W0, out):
 
         def project(s):
             for half in range(2):
-                g_pass = 2 * s + half
                 g_sums = sums_psum.tile([P, PACK, OUT_COLS], F32, tag="sums")
                 for t in range(PACK):
                     mx_pass(s, PACK * half + t, g_sums[:, t, :], w_codes[:], w_scales[:], True, True)
                 copy = nc.vector.tensor_copy if half == 0 else nc.scalar.copy
-                copy(out=g_grouped[:, g_pass, :, :], in_=g_sums[:].rearrange("p t c -> p c t"))
-
-        def quantise_g(s):
+                copy(out=g_grouped[:, 2 * s + half, :, :], in_=g_sums[:].rearrange("p t c -> p c t"))
             cols = slice(2 * s * OUT_COLS, (2 * s + 2) * OUT_COLS)
             nc.vector.quantize_mx(
                 out=g_codes[:, cols].bitcast(FP8X4),
@@ -133,52 +146,71 @@ def tile_gat_pa_t_kernel(tc, x, adj, W0, out):
                 in_=g_grouped[:, 2 * s : 2 * s + 2, :, :].rearrange("p g c t -> p (g c t)"),
             )
 
-        def aggregate(s):
-            block, i = divmod(s - X_SLABS, BLOCK_SLABS)
-            if i == 0:
+        def aggregate(a):
+            first, last = group_of(a)
+            if a == first:
                 sums = sums_psum.tile([P, BLOCK_SLABS, OUT_COLS], F32, tag="sums")
-                sums_of[block] = sums
-            sums = sums_of[block]
+                sums_of[first] = sums
+            acc = sums_of[first][:, a - first, :]
             for c in range(CHUNKS):
                 cols = slice(c * OUT_COLS, (c + 1) * OUT_COLS)
-                mx_pass(s, c, sums[:, i, :], g_codes[:, cols], g_scales[:, cols], c == 0, c == CHUNKS - 1)
-            if i == BLOCK_SLABS - 1:
-                v = sums[:].rearrange("p i c -> p (i c)")
+                mx_pass(
+                    X_SLABS + a, c, acc, g_codes[:, cols], g_scales[:, cols], c == 0, c == CHUNKS - 1
+                )
+            if a == last:
+                width = (last - first + 1) * OUT_COLS
+                v = sums_of[first][:].rearrange("p i c -> p (i c)")[:, 0:width]
                 minus_min = elu_pool.tile([P, BLOCK_SLABS * OUT_COLS], F32)
-                nc.scalar.activation(out=minus_min[:], in_=v, func=ACT.Relu, scale=-1.0)
+                nc.scalar.activation(out=minus_min[:, 0:width], in_=v, func=ACT.Relu, scale=-1.0)
                 exp_min = elu_pool.tile([P, BLOCK_SLABS * OUT_COLS], F32)
-                nc.scalar.activation(out=exp_min[:], in_=minus_min[:], func=ACT.Exp, scale=-1.0)
-                exp_of[block] = exp_min
+                nc.scalar.activation(
+                    out=exp_min[:, 0:width], in_=minus_min[:, 0:width], func=ACT.Exp, scale=-1.0
+                )
+                exp_of[first] = exp_min
 
-        def finish(s):
-            block, i = divmod(s - X_SLABS, BLOCK_SLABS)
-            if i == BLOCK_SLABS - 1:
+        def result_cols(first, last):
+            return slice(first * OUT_COLS, (last + 1) * OUT_COLS)
+
+        def finish(a):
+            first, last = group_of(a)
+            if a == last:
+                width = (last - first + 1) * OUT_COLS
                 nc.vector.scalar_tensor_tensor(
-                    out=results[:, block, :],
-                    in0=exp_of[block][:],
+                    out=results[:, result_cols(first, last)],
+                    in0=exp_of[first][:, 0:width],
                     scalar=-1.0,
-                    in1=sums_of[block][:].rearrange("p i c -> p (i c)"),
+                    in1=sums_of[first][:].rearrange("p i c -> p (i c)")[:, 0:width],
                     op0=ALU.add,
                     op1=ALU.max,
                 )
 
-        def store(block):
-            block_out = out[block * BLOCK_SLABS * P : (block + 1) * BLOCK_SLABS * P, :]
-            nc.sync.dma_start(
-                out=block_out.rearrange("(p i) c -> p (i c)", i=BLOCK_SLABS),
-                in_=results[:, block, :],
-            )
+        def store(a):
+            first, last = group_of(a)
+            if a == last:
+                block = first // BLOCK_SLABS
+                block_out = out[block * BLOCK_SLABS * P : (block + 1) * BLOCK_SLABS * P, :]
+                in_block = slice(
+                    (first - block * BLOCK_SLABS) * OUT_COLS, (last + 1 - block * BLOCK_SLABS) * OUT_COLS
+                )
+                nc.sync.dma_start(
+                    out=block_out.rearrange("(p i) c -> p (i c)", i=BLOCK_SLABS)[:, in_block],
+                    in_=results[:, result_cols(first, last)],
+                )
 
-        w_raw = const.tile([P, 2 * 4, 2 * 32], BF16)
+        w_raw = const.tile([P, HEADS * 2, 2 * HIDDEN], BF16)
         nc.scalar.dma_start(out=w_raw[:], in_=w_view)
         for s in range(ROWS_BUFS):
             load(s)
         ident = const.tile([P, P], F32)
         make_identity(nc, ident[:])
+        table_warmer = const.tile([P, 1], F32)
+        nc.scalar.activation(out=table_warmer[:], in_=ident[:, 0:1], func=ACT.Exp)
         w_grouped = const.tile([P, OUT_COLS, PACK], BF16, align_bytes=64)
-        for h in range(4):
+        for h in range(HEADS):
             nc.vector.tensor_copy(
-                out=w_grouped[:, 32 * h : 32 * (h + 1), :].rearrange("q f (v e) -> q f v e", v=2),
+                out=w_grouped[:, HIDDEN * h : HIDDEN * (h + 1), :].rearrange(
+                    "q f (v e) -> q f v e", v=2
+                ),
                 in_=w_raw[:, 2 * h : 2 * (h + 1), :].rearrange("q v (e f) -> q f v e", e=2),
             )
         w_codes = const.tile([P, OUT_COLS], U32, align_bytes=64)
@@ -191,26 +223,20 @@ def tile_gat_pa_t_kernel(tc, x, adj, W0, out):
         g_grouped = const.tile([P, CHUNKS, OUT_COLS, PACK], BF16, align_bytes=64)
         g_codes = const.tile([P, CHUNKS * OUT_COLS], U32, align_bytes=64)
         g_scales = const.tile([P, CHUNKS * OUT_COLS], U8, align_bytes=64)
-        results = const.tile([P, BLOCKS, BLOCK_SLABS * OUT_COLS], F32)
+        results = const.tile([P, ADJ_SLABS * OUT_COLS], F32)
 
-        for first in range(0, SLABS + 3 * RUN, RUN):
-            for s in range(first, first + RUN):
-                if s < SLABS:
-                    turn(s)
-                    if s + ROWS_BUFS < SLABS:
-                        load(s + ROWS_BUFS)
-                if 0 <= s - RUN < SLABS:
-                    quantise(s - RUN)
-            for s in range(first - 3 * RUN, first - 2 * RUN):
-                if 0 <= s < X_SLABS:
-                    quantise_g(s)
-                elif X_SLABS <= s < SLABS:
-                    finish(s)
-            for s in range(first - 2 * RUN, first - RUN):
-                if 0 <= s < X_SLABS:
+        for first in range(1 - RUN, SLABS + 2 * RUN, RUN):
+            for s in range(max(first, 0), min(first + RUN, SLABS)):
+                turn(s)
+                if s + ROWS_BUFS < SLABS:
+                    load(s + ROWS_BUFS)
+            for s in range(max(first - 1 - RUN, X_SLABS), min(first - 1, SLABS)):
+                finish(s - X_SLABS)
+            for s in range(max(first - 1, 0), min(first - 1 + RUN, SLABS)):
+                if s < X_SLABS:
                     project(s)
-                elif X_SLABS <= s < SLABS:
-                    aggregate(s)
+                else:
+                    aggregate(s - X_SLABS)
 
-        for block in range(BLOCKS):
-            store(block)
+        for a in range(ADJ_SLABS):
+            store(a)

@@ -25,16 +25,14 @@ SLAB_COLS = 4096
 CHUNKS = SLAB_COLS // K_PASS
 BANK_WORDS = 512
 SLAB_BANKS = SLAB_COLS // 2 // BANK_WORDS
-BANK_COLS = SLAB_COLS // SLAB_BANKS
 BANK_CHUNKS = CHUNKS // SLAB_BANKS
 
 X_SLABS = NODES * FEATURES // (P * SLAB_COLS)
 ADJ_SLABS = NODES // P
 SLABS = X_SLABS + ADJ_SLABS
 BLOCK_SLABS = 4
-BLOCKS = ADJ_SLABS // BLOCK_SLABS
 
-RUN = 2
+X_RUN = 2 * FEATURES
 ROWS_BUFS = 10
 
 FLOPS = 2 * NODES * FEATURES * OUT_COLS + 2 * NODES * NODES * OUT_COLS
@@ -55,20 +53,20 @@ def tile_gat_pa_t_kernel(tc, x, adj, W0, out):
     nc = tc.nc
 
     x_view = x.rearrange("(j p e) f -> p j (e f)", p=P, e=2)
-    x_runs = SLAB_COLS // (2 * FEATURES)
     w_view = W0.flatten_outer_dims().rearrange("(c q e) f -> q c (e f)", q=P, e=2)
 
     with ExitStack() as stack:
         const = stack.enter_context(tc.tile_pool(name="const", bufs=1))
         rows_pool = stack.enter_context(tc.tile_pool(name="rows", bufs=ROWS_BUFS))
         grouped_pool = stack.enter_context(tc.tile_pool(name="grouped", bufs=3))
-        codes_pool = stack.enter_context(tc.tile_pool(name="codes", bufs=RUN + 2))
+        codes_pool = stack.enter_context(tc.tile_pool(name="codes", bufs=3))
         elu_pool = stack.enter_context(tc.tile_pool(name="elu", bufs=2))
         turned_psum = stack.enter_context(tc.psum_pool(name="turned", bufs=6))
         sums_psum = stack.enter_context(tc.psum_pool(name="sums", bufs=2))
         stack.enter_context(tc.manual_schedule())
 
         rows_of = {}
+        grouped_of = {}
         codes_of = {}
         scales_of = {}
         sums_of = {}
@@ -77,29 +75,27 @@ def tile_gat_pa_t_kernel(tc, x, adj, W0, out):
         def load(s):
             rows = rows_pool.tile([P, SLAB_COLS], BF16)
             rows_of[s] = rows
-            if s < X_SLABS:
-                nc.sync.dma_start(
-                    out=rows[:].rearrange("p (j c) -> p j c", j=x_runs),
-                    in_=x_view[:, s * x_runs : (s + 1) * x_runs, :],
-                )
-                return
-            block, i = divmod(s - X_SLABS, BLOCK_SLABS)
-            block_rows = adj[block * BLOCK_SLABS * P : (block + 1) * BLOCK_SLABS * P, :]
-            slab_rows = block_rows.rearrange("(p i) k -> p i k", i=BLOCK_SLABS)[:, i, :]
-            pieces = SLAB_BANKS if s == SLABS - 1 else 1
+            pieces = SLAB_BANKS if s == 0 or s == SLABS - 1 else 1
             width = SLAB_COLS // pieces
             for piece in range(pieces):
                 cols = slice(piece * width, (piece + 1) * width)
-                nc.sync.dma_start(out=rows[:, cols], in_=slab_rows[:, cols])
+                if s < X_SLABS:
+                    first_run = (s * SLAB_COLS + piece * width) // X_RUN
+                    nc.sync.dma_start(
+                        out=rows[:, cols].rearrange("p (j c) -> p j c", c=X_RUN),
+                        in_=x_view[:, first_run : first_run + width // X_RUN, :],
+                    )
+                else:
+                    block, i = divmod(s - X_SLABS, BLOCK_SLABS)
+                    block_rows = adj[block * BLOCK_SLABS * P : (block + 1) * BLOCK_SLABS * P, :]
+                    slab_rows = block_rows.rearrange("(p i) k -> p i k", i=BLOCK_SLABS)[:, i, :]
+                    nc.sync.dma_start(out=rows[:, cols], in_=slab_rows[:, cols])
 
         def turn(s):
             words = rows_of[s][:].bitcast(F32)
             grouped = grouped_pool.tile([P, SLAB_COLS], BF16, align_bytes=64)
+            grouped_of[s] = grouped
             grouped_words = grouped[:].bitcast(F32)
-            codes = codes_pool.tile([P, CHUNKS * P], U32, align_bytes=64)
-            scales = codes_pool.tile([P, CHUNKS * P], U8, align_bytes=64)
-            codes_of[s] = codes
-            scales_of[s] = scales
             for b in range(SLAB_BANKS):
                 turned = turned_psum.tile([P, 2 * BANK_CHUNKS, P], F32)
                 for j in range(2 * BANK_CHUNKS):
@@ -112,13 +108,15 @@ def tile_gat_pa_t_kernel(tc, x, adj, W0, out):
                     ),
                     in_=turned[:].rearrange("p (c u) r -> p c r u", u=2),
                 )
-            for b in range(SLAB_BANKS):
-                cols = slice(b * BANK_CHUNKS * P, (b + 1) * BANK_CHUNKS * P)
-                nc.vector.quantize_mx(
-                    out=codes[:, cols].bitcast(FP8X4),
-                    scales=scales[:, cols],
-                    in_=grouped[:, b * BANK_COLS : (b + 1) * BANK_COLS],
-                )
+
+        def quantise(s):
+            codes = codes_pool.tile([P, CHUNKS * P], U32, align_bytes=64)
+            scales = codes_pool.tile([P, CHUNKS * P], U8, align_bytes=64)
+            codes_of[s] = codes
+            scales_of[s] = scales
+            nc.vector.quantize_mx(
+                out=codes[:].bitcast(FP8X4), scales=scales[:], in_=grouped_of[s][:]
+            )
 
         def mx_pass(s, c, acc, rhs_codes, rhs_scales, start, stop):
             cols = slice(c * P, (c + 1) * P)
@@ -225,18 +223,19 @@ def tile_gat_pa_t_kernel(tc, x, adj, W0, out):
         g_scales = const.tile([P, CHUNKS * OUT_COLS], U8, align_bytes=64)
         results = const.tile([P, ADJ_SLABS * OUT_COLS], F32)
 
-        for first in range(1 - RUN, SLABS + 2 * RUN, RUN):
-            for s in range(max(first, 0), min(first + RUN, SLABS)):
-                turn(s)
-                if s + ROWS_BUFS < SLABS:
-                    load(s + ROWS_BUFS)
-            for s in range(max(first - 1 - RUN, X_SLABS), min(first - 1, SLABS)):
-                finish(s - X_SLABS)
-            for s in range(max(first - 1, 0), min(first - 1 + RUN, SLABS)):
-                if s < X_SLABS:
-                    project(s)
-                else:
-                    aggregate(s - X_SLABS)
+        for step in range(SLABS + 3):
+            if step < SLABS:
+                turn(step)
+                if step + ROWS_BUFS < SLABS:
+                    load(step + ROWS_BUFS)
+            if 0 <= step - 1 < SLABS:
+                quantise(step - 1)
+            if X_SLABS <= step - 3 < SLABS:
+                finish(step - 3 - X_SLABS)
+            if 0 <= step - 2 < X_SLABS:
+                project(step - 2)
+            if X_SLABS <= step - 2 < SLABS:
+                aggregate(step - 2 - X_SLABS)
 
         for a in range(ADJ_SLABS):
             store(a)

from contextlib import ExitStack

import concourse.mybir as mybir
from concourse.masks import make_identity

BF16 = mybir.dt.bfloat16
F32 = mybir.dt.float32
U32 = mybir.dt.uint32
U8 = mybir.dt.uint8
FP8X4 = mybir.dt.float8_e4m3fn_x4
ACT = mybir.ActivationFunctionType
ALU = mybir.AluOpType

P = 128
PACK = 4
K_PASS = P * PACK

NODES = 4096
FEATURES = 512
HEADS = 4
HIDDEN = 32
OUT_COLS = HEADS * HIDDEN

SLAB_COLS = 4096
CHUNKS = SLAB_COLS // K_PASS
BANK_WORDS = 512
SLAB_BANKS = SLAB_COLS // 2 // BANK_WORDS
BANK_CHUNKS = CHUNKS // SLAB_BANKS

X_SLABS = NODES * FEATURES // (P * SLAB_COLS)
ADJ_SLABS = NODES // P
SLABS = X_SLABS + ADJ_SLABS
BLOCK_SLABS = 4

X_RUN = 2 * FEATURES
ROWS_BUFS = 10

FLOPS = 2 * NODES * FEATURES * OUT_COLS + 2 * NODES * NODES * OUT_COLS


def group_of(a):
    first = a - a % BLOCK_SLABS
    last = first + BLOCK_SLABS - 1
    if last == ADJ_SLABS - 1:
        if a == last:
            first = last
        else:
            last = last - 1
    return first, last


def tile_gat_pa_t_kernel(tc, x, adj, W0, out):
    nc = tc.nc

    x_view = x.rearrange("(j p e) f -> p j (e f)", p=P, e=2)
    w_view = W0.flatten_outer_dims().rearrange("(c q e) f -> q c (e f)", q=P, e=2)

    with ExitStack() as stack:
        const = stack.enter_context(tc.tile_pool(name="const", bufs=1))
        rows_pool = stack.enter_context(tc.tile_pool(name="rows", bufs=ROWS_BUFS))
        grouped_pool = stack.enter_context(tc.tile_pool(name="grouped", bufs=3))
        codes_pool = stack.enter_context(tc.tile_pool(name="codes", bufs=3))
        elu_pool = stack.enter_context(tc.tile_pool(name="elu", bufs=2))
        turned_psum = stack.enter_context(tc.psum_pool(name="turned", bufs=6))
        sums_psum = stack.enter_context(tc.psum_pool(name="sums", bufs=2))
        stack.enter_context(tc.manual_schedule())

        rows_of = {}
        grouped_of = {}
        codes_of = {}
        scales_of = {}
        sums_of = {}
        exp_of = {}

        def load(s):
            rows = rows_pool.tile([P, SLAB_COLS], BF16)
            rows_of[s] = rows
            pieces = SLAB_BANKS if s == 0 or s == SLABS - 1 else 1
            width = SLAB_COLS // pieces
            for piece in range(pieces):
                cols = slice(piece * width, (piece + 1) * width)
                if s < X_SLABS:
                    first_run = (s * SLAB_COLS + piece * width) // X_RUN
                    nc.sync.dma_start(
                        out=rows[:, cols].rearrange("p (j c) -> p j c", c=X_RUN),
                        in_=x_view[:, first_run : first_run + width // X_RUN, :],
                    )
                else:
                    block, i = divmod(s - X_SLABS, BLOCK_SLABS)
                    block_rows = adj[block * BLOCK_SLABS * P : (block + 1) * BLOCK_SLABS * P, :]
                    slab_rows = block_rows.rearrange("(p i) k -> p i k", i=BLOCK_SLABS)[:, i, :]
                    nc.sync.dma_start(out=rows[:, cols], in_=slab_rows[:, cols])

        def turn(s):
            words = rows_of[s][:].bitcast(F32)
            grouped = grouped_pool.tile([P, SLAB_COLS], BF16, align_bytes=64)
            grouped_of[s] = grouped
            grouped_words = grouped[:].bitcast(F32)
            for b in range(SLAB_BANKS):
                turned = turned_psum.tile([P, 2 * BANK_CHUNKS, P], F32)
                for j in range(2 * BANK_CHUNKS):
                    first = (b * 2 * BANK_CHUNKS + j) * P
                    nc.tensor.transpose(turned[:, j, :], words[:, first : first + P], ident[:])
                copy = nc.vector.tensor_copy if b == 0 else nc.scalar.copy
                copy(
                    out=grouped_words[:, b * BANK_WORDS : (b + 1) * BANK_WORDS].rearrange(
                        "p (c r u) -> p c r u", c=BANK_CHUNKS, u=2
                    ),
                    in_=turned[:].rearrange("p (c u) r -> p c r u", u=2),
                )

        def quantise(s):
            codes = codes_pool.tile([P, CHUNKS * P], U32, align_bytes=64)
            scales = codes_pool.tile([P, CHUNKS * P], U8, align_bytes=64)
            codes_of[s] = codes
            scales_of[s] = scales
            nc.vector.quantize_mx(
                out=codes[:].bitcast(FP8X4), scales=scales[:], in_=grouped_of[s][:]
            )

        def mx_pass(s, c, acc, rhs_codes, rhs_scales, start, stop):
            cols = slice(c * P, (c + 1) * P)
            nc.tensor.matmul_mx(
                out=acc,
                lhsT=codes_of[s][:, cols].bitcast(FP8X4),
                lhsT_scale=scales_of[s][:, cols],
                rhs=rhs_codes.bitcast(FP8X4),
                rhs_scale=rhs_scales,
                start=start,
                stop=stop,
            )

        def project(s):
            for half in range(2):
                g_sums = sums_psum.tile([P, PACK, OUT_COLS], F32, tag="sums")
                for t in range(PACK):
                    mx_pass(s, PACK * half + t, g_sums[:, t, :], w_codes[:], w_scales[:], True, True)
                copy = nc.vector.tensor_copy if half == 0 else nc.scalar.copy
                copy(out=g_grouped[:, 2 * s + half, :, :], in_=g_sums[:].rearrange("p t c -> p c t"))
            cols = slice(2 * s * OUT_COLS, (2 * s + 2) * OUT_COLS)
            nc.vector.quantize_mx(
                out=g_codes[:, cols].bitcast(FP8X4),
                scales=g_scales[:, cols],
                in_=g_grouped[:, 2 * s : 2 * s + 2, :, :].rearrange("p g c t -> p (g c t)"),
            )

        def aggregate(a):
            first, last = group_of(a)
            if a == first:
                sums = sums_psum.tile([P, BLOCK_SLABS, OUT_COLS], F32, tag="sums")
                sums_of[first] = sums
            acc = sums_of[first][:, a - first, :]
            for c in range(CHUNKS):
                cols = slice(c * OUT_COLS, (c + 1) * OUT_COLS)
                mx_pass(
                    X_SLABS + a, c, acc, g_codes[:, cols], g_scales[:, cols], c == 0, c == CHUNKS - 1
                )
            if a == last:
                width = (last - first + 1) * OUT_COLS
                v = sums_of[first][:].rearrange("p i c -> p (i c)")[:, 0:width]
                minus_min = elu_pool.tile([P, BLOCK_SLABS * OUT_COLS], F32)
                nc.scalar.activation(out=minus_min[:, 0:width], in_=v, func=ACT.Relu, scale=-1.0)
                exp_min = elu_pool.tile([P, BLOCK_SLABS * OUT_COLS], F32)
                nc.scalar.activation(
                    out=exp_min[:, 0:width], in_=minus_min[:, 0:width], func=ACT.Exp, scale=-1.0
                )
                exp_of[first] = exp_min

        def result_cols(first, last):
            return slice(first * OUT_COLS, (last + 1) * OUT_COLS)

        def finish(a):
            first, last = group_of(a)
            if a == last:
                width = (last - first + 1) * OUT_COLS
                nc.vector.scalar_tensor_tensor(
                    out=results[:, result_cols(first, last)],
                    in0=exp_of[first][:, 0:width],
                    scalar=-1.0,
                    in1=sums_of[first][:].rearrange("p i c -> p (i c)")[:, 0:width],
                    op0=ALU.add,
                    op1=ALU.max,
                )

        def store(a):
            first, last = group_of(a)
            if a == last:
                block = first // BLOCK_SLABS
                block_out = out[block * BLOCK_SLABS * P : (block + 1) * BLOCK_SLABS * P, :]
                in_block = slice(
                    (first - block * BLOCK_SLABS) * OUT_COLS, (last + 1 - block * BLOCK_SLABS) * OUT_COLS
                )
                nc.sync.dma_start(
                    out=block_out.rearrange("(p i) c -> p (i c)", i=BLOCK_SLABS)[:, in_block],
                    in_=results[:, result_cols(first, last)],
                )

        w_raw = const.tile([P, HEADS * 2, 2 * HIDDEN], BF16)
        nc.scalar.dma_start(out=w_raw[:], in_=w_view)
        for s in range(ROWS_BUFS):
            load(s)
        ident = const.tile([P, P], F32)
        make_identity(nc, ident[:])
        table_warmer = const.tile([P, 1], F32)
        nc.scalar.activation(out=table_warmer[:], in_=ident[:, 0:1], func=ACT.Exp)
        w_grouped = const.tile([P, OUT_COLS, PACK], BF16, align_bytes=64)
        for h in range(HEADS):
            nc.vector.tensor_copy(
                out=w_grouped[:, HIDDEN * h : HIDDEN * (h + 1), :].rearrange(
                    "q f (v e) -> q f v e", v=2
                ),
                in_=w_raw[:, 2 * h : 2 * (h + 1), :].rearrange("q v (e f) -> q f v e", e=2),
            )
        w_codes = const.tile([P, OUT_COLS], U32, align_bytes=64)
        w_scales = const.tile([P, OUT_COLS], U8, align_bytes=64)
        nc.vector.quantize_mx(
            out=w_codes[:].bitcast(FP8X4),
            scales=w_scales[:],
            in_=w_grouped[:].rearrange("q c t -> q (c t)"),
        )
        g_grouped = const.tile([P, CHUNKS, OUT_COLS, PACK], BF16, align_bytes=64)
        g_codes = const.tile([P, CHUNKS * OUT_COLS], U32, align_bytes=64)
        g_scales = const.tile([P, CHUNKS * OUT_COLS], U8, align_bytes=64)
        results = const.tile([P, ADJ_SLABS * OUT_COLS], F32)

        for step in range(SLABS + 3):
            if step < SLABS:
                turn(step)
                if step + ROWS_BUFS < SLABS:
                    load(step + ROWS_BUFS)
            if 0 <= step - 1 < SLABS:
                quantise(step - 1)
            if X_SLABS <= step - 3 < SLABS:
                finish(step - 3 - X_SLABS)
            if 0 <= step - 2 < X_SLABS:
                project(step - 2)
            if X_SLABS <= step - 2 < SLABS:
                aggregate(step - 2 - X_SLABS)

        for a in range(ADJ_SLABS):
            store(a)
